import numpy as np
import ml_dtypes


def mxq(x, axis, fmt="e4m3"):
    dtype, down = {"e4m3": (ml_dtypes.float8_e4m3fn, 7), "e5m2": (ml_dtypes.float8_e5m2, 14)}[fmt]
    v = np.moveaxis(np.asarray(x, np.float32).astype(ml_dtypes.bfloat16).astype(np.float64), axis, -1)
    blocks = v.reshape(v.shape[:-1] + (-1, 32))
    amax = np.abs(blocks).max(-1, keepdims=True)
    byte = np.maximum(np.where(amax > 0, np.frexp(amax)[1] - 1 + 127, 0) - down, 1)
    scale = np.exp2(byte - 127.0)
    codes = (blocks / scale).astype(np.float32).astype(dtype).astype(np.float64)
    return np.moveaxis((codes * scale).reshape(v.shape), -1, axis)


WIDE = False


def mx_kscale(k):
    if not WIDE:
        return np.ones(k)
    levels = np.array([20, -20, 10, -10, 0])
    a = np.random.permutation(np.resize(levels, k // 512 * 4)).reshape(k // 512, 4)
    idx = np.arange(k)
    return np.exp2(a[idx // 512, idx % 128 // 32])


BF16 = ml_dtypes.bfloat16


def bf(x):
    return np.asarray(x, np.float32).astype(BF16)


def f64(x):
    return np.asarray(x).astype(np.float64)


U1, U2, BATCH = 256, 512, 1024
K = (U1 + U2) * 3
N = U2 * 3
PROBS = [[1.0, 0.5, 0.0, 1.0, 0.5, 0.0], [0.5, 0.75, 0.5, 0.5, 0.75, 0.5], [0.0, 0.5, 1.0, 0.0, 0.5, 1.0]]
EDGES = [0, U1, 2 * U1, 3 * U1, 3 * U1 + U2, 3 * U1 + 2 * U2, 3 * U1 + 3 * U2]


def build_mask():
    p = np.zeros((N, K))
    for ub in range(len(PROBS)):
        for j in range(len(PROBS[ub])):
            p[ub * U2:(ub + 1) * U2, EDGES[j]:EDGES[j + 1]] = PROBS[ub][j]
    return (np.random.random((N, K)) < p).astype(np.float64)


def setup_inputs():
    u = mx_kscale(N)
    x = np.random.standard_normal((BATCH, K))
    w = np.random.uniform(0.0, 2.5 / np.sqrt(K), (K, N)) / u
    b = np.random.standard_normal(N) * 0.3
    mask = build_mask()
    g = np.random.standard_normal((BATCH, N)) * np.exp2(np.random.randint(-12, 1, (BATCH, 1))) * 16.0 * u
    return {"x": bf(x), "w": bf(w), "b": bf(b), "mask": bf(mask), "grad_out": bf(g)}


def reference(x, w, b, mask, grad_out):
    wm = f64(mask).T * f64(w)
    gq = mxq(f64(grad_out), 1, "e5m2")
    out = np.zeros((BATCH, K))
    for j in range(len(EDGES) - 1):
        used = [ub for ub in range(len(PROBS)) if PROBS[ub][j] > 0.0]
        lo, hi = used[0] * U2, (used[-1] + 1) * U2
        r = slice(EDGES[j], EDGES[j + 1])
        out[:, r] = gq[:, lo:hi] @ mxq(wm[r, lo:hi], 1, "e4m3").T
    return out

@@ -1,0 +1,241 @@
+from contextlib import ExitStack
+
+import concourse.masks as masks
+import concourse.mybir as mybir
+
+BF16 = mybir.dt.bfloat16
+F32 = mybir.dt.float32
+I32 = mybir.dt.int32
+U32 = mybir.dt.uint32
+U8 = mybir.dt.uint8
+E4X4 = mybir.dt.float8_e4m3fn_x4
+E5X4 = mybir.dt.float8_e5m2_x4
+
+P = 128
+ROWS = 1024
+UNITS = 1536
+INPUTS = 2304
+RT = ROWS // P
+FLOPS = 2 * ROWS * 2752512
+BYTES = 2 * ROWS * UNITS + 2 * 2 * 2752512 + 4 * ROWS * INPUTS
+
+BLOCKS = [
+    (0, 256, 0, 1024),
+    (256, 512, 0, 1536),
+    (512, 768, 512, 1536),
+    (768, 1280, 0, 1024),
+    (1280, 1792, 0, 1536),
+    (1792, 2304, 512, 1536),
+]
+MASK_W = [1536, 2304, 1536]
+CODE_W = [1536, 2304, 1792]
+
+
+def mask_col(c, i):
+    if c == 0:
+        return i if i < 512 else i - 256
+    if c == 1:
+        return i
+    return i - 256 if i < 768 else i - 768
+
+
+def code_col(c, i):
+    if c == 0:
+        return i if i < 512 else i - 256
+    if c == 1:
+        return i
+    return i if i < 768 else i - 512
+
+
+def tile_gpi_t_kernel(tc, x, w, b, mask, grad_out, out):
+    nc = tc.nc
+    with ExitStack() as ctx:
+        keep = ctx.enter_context(tc.tile_pool(name="keep", bufs=1))
+        big = ctx.enter_context(tc.tile_pool(name="big", bufs=8))
+        grp = ctx.enter_context(tc.tile_pool(name="grp", bufs=3))
+        tp = ctx.enter_context(tc.psum_pool(name="tp", bufs=4))
+        accp = ctx.enter_context(tc.psum_pool(name="accp", bufs=4))
+
+        ident = keep.tile([P, P], F32, name="ident", tag="ident")
+        masks.make_identity(nc, ident[:])
+
+        w_sb = [
+            keep.tile([P, (i1 - i0) // P, u1 - u0], BF16, name="w%d" % n, tag="w%d" % n)
+            for n, (i0, i1, u0, u1) in enumerate(BLOCKS)
+        ]
+        m_sb = [
+            keep.tile([P, 2, 2, MASK_W[c]], BF16, name="m%d" % c, tag="m%d" % c)
+            for c in range(3)
+        ]
+        wcodes = [
+            keep.tile([P, CODE_W[c]], U32, name="wc%d" % c, tag="wc%d" % c, align_bytes=64)
+            for c in range(3)
+        ]
+        wscales = [
+            keep.tile([P, CODE_W[c]], U8, name="ws%d" % c, tag="ws%d" % c, align_bytes=64)
+            for c in range(3)
+        ]
+        gcodes = keep.tile([P, 3, ROWS], U32, name="gcodes", tag="gcodes", align_bytes=64)
+        gscales = keep.tile([P, 3, ROWS], U8, name="gscales", tag="gscales", align_bytes=64)
+        xstage = [
+            keep.tile([P, 768], F32, name="xs%d" % t, tag="xs%d" % t) for t in range(RT)
+        ]
+
+        nc.vector.memset(wcodes[2][:, 0:256].bitcast(I32), 0)
+        nc.vector.memset(wscales[2][:, 0:256].bitcast(I32), 0)
+
+        g_view = grad_out.rearrange("(p t) u -> p t u", t=RT)
+        out_view = out.rearrange("(p t) i -> p t i", t=RT)
+
+        def load_w(n):
+            i0, i1, u0, u1 = BLOCKS[n]
+            nc.sync.dma_start(
+                out=w_sb[n][:], in_=w[i0:i1, u0:u1].rearrange("(s p) u -> p s u", p=P)
+            )
+
+        def load_mask(c, i0, i1):
+            m0 = mask_col(c, i0)
+            for u in range(2):
+                r0 = 512 * c + 256 * u
+                nc.sync.dma_start(
+                    out=m_sb[c][:, u, :, m0 : m0 + i1 - i0],
+                    in_=mask[r0 : r0 + 256, i0:i1].rearrange("(q e) i -> q e i", e=2),
+                )
+
+        g_sb = []
+
+        def load_g(pair):
+            gt = big.tile([P, 2, UNITS], BF16, name="g%d" % pair, tag="big")
+            nc.sync.dma_start(out=gt[:], in_=g_view[:, 2 * pair : 2 * pair + 2, :])
+            g_sb.append(gt)
+
+        load_w(3)
+        load_mask(0, 768, 1280)
+        load_mask(1, 768, 1280)
+        for pair in range(4):
+            load_g(pair)
+        load_w(4)
+        load_mask(0, 1280, 1792)
+        load_mask(1, 1280, 2304)
+        load_mask(2, 1280, 2304)
+        load_w(5)
+        load_w(2)
+        load_w(1)
+        load_mask(2, 256, 768)
+        load_mask(1, 0, 768)
+        load_w(0)
+        load_mask(0, 0, 512)
+
+        def w_words(i):
+            for n, (i0, i1, u0, u1) in enumerate(BLOCKS):
+                if i0 <= i < i1:
+                    return w_sb[n][:, (i - i0) // P, :].bitcast(F32), u0 // 2
+            raise ValueError("no block")
+
+        def prep_w(c, i0, n):
+            wg = grp.tile([P, 2048], BF16, name="wg", tag="wg", align_bytes=64)
+            for h in range(n // 256):
+                bank = tp.tile([P, 512], F32, name="wbank", tag="tp")
+                for s in range(2):
+                    words, first = w_words(i0 + 256 * h + P * s)
+                    for u in range(2):
+                        k0 = 256 * c + P * u - first
+                        nc.tensor.transpose(
+                            bank[:, 256 * u + P * s : 256 * u + P * s + P],
+                            words[:, k0 : k0 + P],
+                            ident[:],
+                        )
+                m0 = mask_col(c, i0 + 256 * h)
+                nc.vector.tensor_tensor(
+                    out=wg[:, 1024 * h : 1024 * h + 1024].rearrange(
+                        "q (i u e) -> q i u e", u=2, e=2
+                    ),
+                    in0=bank[:].bitcast(BF16).rearrange("q (u i e) -> q i u e", u=2, e=2),
+                    in1=m_sb[c][:, :, :, m0 : m0 + 256].rearrange("q u e i -> q i u e"),
+                    op=mybir.AluOpType.mult,
+                )
+            c0 = code_col(c, i0)
+            nc.vector.quantize_mx(
+                out=wcodes[c][:, c0 : c0 + n].bitcast(E4X4),
+                scales=wscales[c][:, c0 : c0 + n],
+                in_=wg[:, 0 : 4 * n],
+            )
+
+        def prep_g(pair, c):
+            bank = tp.tile([P, 512], F32, name="gbank", tag="tp")
+            for tt in range(2):
+                words = g_sb[pair][:, tt, :].bitcast(F32)
+                for u in range(2):
+                    k0 = 256 * c + P * u
+                    nc.tensor.transpose(
+                        bank[:, 256 * u + P * tt : 256 * u + P * tt + P],
+                        words[:, k0 : k0 + P],
+                        ident[:],
+                    )
+            gg = grp.tile([P, 512], F32, name="gg", tag="gg", align_bytes=64)
+            nc.scalar.copy(
+                out=gg[:].rearrange("q (j u) -> q j u", u=2),
+                in_=bank[:].rearrange("q (u j) -> q j u", u=2),
+            )
+            nc.vector.quantize_mx(
+                out=gcodes[:, c, 256 * pair : 256 * pair + 256].bitcast(E5X4),
+                scales=gscales[:, c, 256 * pair : 256 * pair + 256],
+                in_=gg[:].bitcast(BF16),
+            )
+
+        def mx(passes, t, dst):
+            acc = accp.tile([P, 512], F32, name="acc", tag="acc")
+            for k, (c, col) in enumerate(passes):
+                nc.tensor.matmul_mx(
+                    out=acc[:],
+                    lhsT=gcodes[:, c, P * t : P * t + P].bitcast(E5X4),
+                    lhsT_scale=gscales[:, c, P * t : P * t + P],
+                    rhs=wcodes[c][:, col : col + 512].bitcast(E4X4),
+                    rhs_scale=wscales[c][:, col : col + 512],
+                    start=(k == 0),
+                    stop=(k == len(passes) - 1),
+                )
+            nc.scalar.copy(out=dst, in_=acc[:, 0 : dst.shape[1]])
+
+        T_A = [(0, 0), (1, 0), (2, 0)]
+        T_B = [(1, 512), (2, 512)]
+        T_C = [(0, 512), (1, 768)]
+        T_D = [(0, 1024), (1, 1280), (2, 768)]
+        T_E = [(1, 1792), (2, 1280)]
+
+        ystage = []
+
+        prep_w(0, 768, 512)
+        prep_w(1, 768, 512)
+        for pair in range(4):
+            for c in range(3):
+                prep_g(pair, c)
+            for t in (2 * pair, 2 * pair + 1):
+                ys = big.tile([P, 1536], F32, name="ys%d" % t, tag="big")
+                ystage.append(ys)
+                mx(T_C, t, ys[:, 0:512])
+        prep_w(0, 1280, 512)
+        prep_w(1, 1280, 512)
+        prep_w(2, 1280, 512)
+        for t in range(RT):
+            if t == 2:
+                prep_w(1, 1792, 512)
+            if t == 5:
+                prep_w(2, 1792, 512)
+            mx(T_D, t, ystage[t][:, 512:1024])
+        for t in range(RT):
+            if t == 2:
+                prep_w(2, 256, 512)
+            if t == 5:
+                prep_w(1, 512, 256)
+            mx(T_E, t, ystage[t][:, 1024:1536])
+            nc.sync.dma_start(out=out_view[:, t, 768:2304], in_=ystage[t][:])
+        for t in range(RT):
+            if t == 2:
+                prep_w(0, 0, 512)
+            if t == 5:
+                prep_w(1, 0, 512)
+            mx(T_B, t, xstage[t][:, 512:768])
+        for t in range(RT):
+            mx(T_A, t, xstage[t][:, 0:512])
+            nc.sync.dma_start(out=out_view[:, t, 0:768], in_=xstage[t][:])

@@ -53,7 +53,7 @@ def tile_gpi_t_kernel(tc, x, w, b, mask, grad_out, out):
         keep = ctx.enter_context(tc.tile_pool(name="keep", bufs=1))
         big = ctx.enter_context(tc.tile_pool(name="big", bufs=8))
         grp = ctx.enter_context(tc.tile_pool(name="grp", bufs=3))
-        tp = ctx.enter_context(tc.psum_pool(name="tp", bufs=4))
+        tp = ctx.enter_context(tc.psum_pool(name="tp", bufs=2))
         accp = ctx.enter_context(tc.psum_pool(name="accp", bufs=4))
 
         ident = keep.tile([P, P], F32, name="ident", tag="ident")
@@ -134,8 +134,9 @@ def tile_gpi_t_kernel(tc, x, w, b, mask, grad_out, out):
 
         def prep_w(c, i0, n):
             wg = grp.tile([P, 2048], BF16, name="wg", tag="wg", align_bytes=64)
+            banks = tp.tile([P, 2, 512], F32, name="wbanks", tag="tp")
             for h in range(n // 256):
-                bank = tp.tile([P, 512], F32, name="wbank", tag="tp")
+                bank = banks[:, h, :]
                 for s in range(2):
                     words, first = w_words(i0 + 256 * h + P * s)
                     for u in range(2):
@@ -145,12 +146,14 @@ def tile_gpi_t_kernel(tc, x, w, b, mask, grad_out, out):
                             words[:, k0 : k0 + P],
                             ident[:],
                         )
+            for h in range(n // 256):
+                bank = banks[:, h, :]
                 m0 = mask_col(c, i0 + 256 * h)
                 nc.vector.tensor_tensor(
                     out=wg[:, 1024 * h : 1024 * h + 1024].rearrange(
                         "q (i u e) -> q i u e", u=2, e=2
                     ),
-                    in0=bank[:].bitcast(BF16).rearrange("q (u i e) -> q i u e", u=2, e=2),
+                    in0=bank.bitcast(BF16).rearrange("q (u i e) -> q i u e", u=2, e=2),
                     in1=m_sb[c][:, :, :, m0 : m0 + 256].rearrange("q u e i -> q i u e"),
                     op=mybir.AluOpType.mult,
                 )
@@ -161,26 +164,28 @@ def tile_gpi_t_kernel(tc, x, w, b, mask, grad_out, out):
                 in_=wg[:, 0 : 4 * n],
             )
 
-        def prep_g(pair, c):
-            bank = tp.tile([P, 512], F32, name="gbank", tag="tp")
-            for tt in range(2):
-                words = g_sb[pair][:, tt, :].bitcast(F32)
-                for u in range(2):
-                    k0 = 256 * c + P * u
-                    nc.tensor.transpose(
-                        bank[:, 256 * u + P * tt : 256 * u + P * tt + P],
-                        words[:, k0 : k0 + P],
-                        ident[:],
-                    )
-            gg = grp.tile([P, 512], F32, name="gg", tag="gg", align_bytes=64)
-            nc.scalar.copy(
-                out=gg[:].rearrange("q (j u) -> q j u", u=2),
-                in_=bank[:].rearrange("q (u j) -> q j u", u=2),
-            )
+        def prep_g(j, c):
+            banks = tp.tile([P, 2, 512], F32, name="gbanks", tag="tp")
+            for h in range(2):
+                for tt in range(2):
+                    words = g_sb[2 * j + h][:, tt, :].bitcast(F32)
+                    for u in range(2):
+                        k0 = 256 * c + P * u
+                        nc.tensor.transpose(
+                            banks[:, h, 256 * u + P * tt : 256 * u + P * tt + P],
+                            words[:, k0 : k0 + P],
+                            ident[:],
+                        )
+            gg = grp.tile([P, 2, 512], F32, name="gg", tag="gg", align_bytes=64)
+            for h in range(2):
+                nc.scalar.copy(
+                    out=gg[:, h, :].rearrange("q (j u) -> q j u", u=2),
+                    in_=banks[:, h, :].rearrange("q (u j) -> q j u", u=2),
+                )
             nc.vector.quantize_mx(
-                out=gcodes[:, c, 256 * pair : 256 * pair + 256].bitcast(E5X4),
-                scales=gscales[:, c, 256 * pair : 256 * pair + 256],
-                in_=gg[:].bitcast(BF16),
+                out=gcodes[:, c, 512 * j : 512 * j + 512].bitcast(E5X4),
+                scales=gscales[:, c, 512 * j : 512 * j + 512],
+                in_=gg[:].rearrange("q h j -> q (h j)").bitcast(BF16),
             )
 
         def mx(passes, t, dst):
@@ -207,13 +212,14 @@ def tile_gpi_t_kernel(tc, x, w, b, mask, grad_out, out):
 
         prep_w(0, 768, 512)
         prep_w(1, 768, 512)
-        for pair in range(4):
+        for j in range(2):
             for c in range(3):
-                prep_g(pair, c)
-            for t in (2 * pair, 2 * pair + 1):
+                prep_g(j, c)
+            for t in range(4 * j, 4 * j + 4):
                 ys = big.tile([P, 1536], F32, name="ys%d" % t, tag="big")
                 ystage.append(ys)
                 mx(T_C, t, ys[:, 0:512])
+                nc.sync.dma_start(out=out_view[:, t, 768:1280], in_=ys[:, 0:512])
         prep_w(0, 1280, 512)
         prep_w(1, 1280, 512)
         prep_w(2, 1280, 512)
@@ -223,13 +229,14 @@ def tile_gpi_t_kernel(tc, x, w, b, mask, grad_out, out):
             if t == 5:
                 prep_w(2, 1792, 512)
             mx(T_D, t, ystage[t][:, 512:1024])
+            nc.sync.dma_start(out=out_view[:, t, 1280:1792], in_=ystage[t][:, 512:1024])
         for t in range(RT):
             if t == 2:
                 prep_w(2, 256, 512)
             if t == 5:
                 prep_w(1, 512, 256)
             mx(T_E, t, ystage[t][:, 1024:1536])
-            nc.sync.dma_start(out=out_view[:, t, 768:2304], in_=ystage[t][:])
+            nc.sync.dma_start(out=out_view[:, t, 1792:2304], in_=ystage[t][:, 1024:1536])
         for t in range(RT):
             if t == 2:
                 prep_w(0, 0, 512)

@@ -28,7 +28,23 @@ BLOCKS = [
     (1792, 2304, 512, 1536),
 ]
 MASK_W = [1536, 2304, 1536]
-CODE_W = [1536, 2304, 1792]
+CODE_W = [1536, 2560, 1536]
+
+TILES = {
+    "C": [(0, 512), (1, 1024)],
+    "X2": [(1, 512), (2, 0)],
+    "E": [(1, 2048), (2, 1024)],
+    "D": [(0, 1024), (1, 1536), (2, 512)],
+    "X1": [(1, 0), (0, 0)],
+}
+TILE_ORDER = ["C", "X2", "E", "D", "X1"]
+W_BEFORE = {
+    2: [(2, 256, 512), (1, 512, 256)],
+    7: [(1, 1792, 512), (2, 1792, 512)],
+    14: [(0, 1280, 512), (1, 1280, 512)],
+    20: [(2, 1280, 512), (1, 0, 512)],
+    24: [(0, 0, 512)],
+}
 
 
 def mask_col(c, i):
@@ -40,11 +56,9 @@ def mask_col(c, i):
 
 
 def code_col(c, i):
-    if c == 0:
-        return i if i < 512 else i - 256
     if c == 1:
-        return i
-    return i if i < 768 else i - 512
+        return i if i < 512 else i + 256
+    return mask_col(c, i)
 
 
 def tile_gpi_t_kernel(tc, x, w, b, mask, grad_out, out):
@@ -53,8 +67,9 @@ def tile_gpi_t_kernel(tc, x, w, b, mask, grad_out, out):
         keep = ctx.enter_context(tc.tile_pool(name="keep", bufs=1))
         big = ctx.enter_context(tc.tile_pool(name="big", bufs=8))
         grp = ctx.enter_context(tc.tile_pool(name="grp", bufs=3))
-        tp = ctx.enter_context(tc.psum_pool(name="tp", bufs=2))
+        tp = ctx.enter_context(tc.psum_pool(name="tp", bufs=4))
         accp = ctx.enter_context(tc.psum_pool(name="accp", bufs=4))
+        ctx.enter_context(tc.manual_schedule())
 
         ident = keep.tile([P, P], F32, name="ident", tag="ident")
         masks.make_identity(nc, ident[:])
@@ -78,11 +93,11 @@ def tile_gpi_t_kernel(tc, x, w, b, mask, grad_out, out):
         gcodes = keep.tile([P, 3, ROWS], U32, name="gcodes", tag="gcodes", align_bytes=64)
         gscales = keep.tile([P, 3, ROWS], U8, name="gscales", tag="gscales", align_bytes=64)
         xstage = [
-            keep.tile([P, 768], F32, name="xs%d" % t, tag="xs%d" % t) for t in range(RT)
+            keep.tile([P, 4, 256], F32, name="xs%d" % t, tag="xs%d" % t) for t in range(RT)
         ]
 
-        nc.vector.memset(wcodes[2][:, 0:256].bitcast(I32), 0)
-        nc.vector.memset(wscales[2][:, 0:256].bitcast(I32), 0)
+        nc.vector.memset(wcodes[1][:, 512:768].bitcast(I32), 0)
+        nc.vector.memset(wscales[1][:, 512:768].bitcast(I32), 0)
 
         g_view = grad_out.rearrange("(p t) u -> p t u", t=RT)
         out_view = out.rearrange("(p t) i -> p t i", t=RT)
@@ -114,16 +129,19 @@ def tile_gpi_t_kernel(tc, x, w, b, mask, grad_out, out):
         load_mask(1, 768, 1280)
         for pair in range(4):
             load_g(pair)
-        load_w(4)
-        load_mask(0, 1280, 1792)
-        load_mask(1, 1280, 2304)
-        load_mask(2, 1280, 2304)
-        load_w(5)
         load_w(2)
         load_w(1)
         load_mask(2, 256, 768)
-        load_mask(1, 0, 768)
+        load_mask(1, 512, 768)
+        load_w(5)
+        load_mask(1, 1792, 2304)
+        load_mask(2, 1792, 2304)
+        load_w(4)
+        load_mask(0, 1280, 1792)
+        load_mask(1, 1280, 1792)
+        load_mask(2, 1280, 1792)
         load_w(0)
+        load_mask(1, 0, 512)
         load_mask(0, 0, 512)
 
         def w_words(i):
@@ -132,31 +150,7 @@ def tile_gpi_t_kernel(tc, x, w, b, mask, grad_out, out):
                     return w_sb[n][:, (i - i0) // P, :].bitcast(F32), u0 // 2
             raise ValueError("no block")
 
-        def prep_w(c, i0, n):
-            wg = grp.tile([P, 2048], BF16, name="wg", tag="wg", align_bytes=64)
-            banks = tp.tile([P, 2, 512], F32, name="wbanks", tag="tp")
-            for h in range(n // 256):
-                bank = banks[:, h, :]
-                for s in range(2):
-                    words, first = w_words(i0 + 256 * h + P * s)
-                    for u in range(2):
-                        k0 = 256 * c + P * u - first
-                        nc.tensor.transpose(
-                            bank[:, 256 * u + P * s : 256 * u + P * s + P],
-                            words[:, k0 : k0 + P],
-                            ident[:],
-                        )
-            for h in range(n // 256):
-                bank = banks[:, h, :]
-                m0 = mask_col(c, i0 + 256 * h)
-                nc.vector.tensor_tensor(
-                    out=wg[:, 1024 * h : 1024 * h + 1024].rearrange(
-                        "q (i u e) -> q i u e", u=2, e=2
-                    ),
-                    in0=bank.bitcast(BF16).rearrange("q (u i e) -> q i u e", u=2, e=2),
-                    in1=m_sb[c][:, :, :, m0 : m0 + 256].rearrange("q u e i -> q i u e"),
-                    op=mybir.AluOpType.mult,
-                )
+        def quantise_w(c, i0, n, wg):
             c0 = code_col(c, i0)
             nc.vector.quantize_mx(
                 out=wcodes[c][:, c0 : c0 + n].bitcast(E4X4),
@@ -164,23 +158,57 @@ def tile_gpi_t_kernel(tc, x, w, b, mask, grad_out, out):
                 in_=wg[:, 0 : 4 * n],
             )
 
+        def prep_w(units):
+            banks = []
+            for c, i0, n in units:
+                for h in range(n // 256):
+                    bank = tp.tile([P, 512], F32, name="wbank", tag="tp")
+                    banks.append(bank)
+                    for s in range(2):
+                        words, first = w_words(i0 + 256 * h + P * s)
+                        for u in range(2):
+                            k0 = 256 * c + P * u - first
+                            nc.tensor.transpose(
+                                bank[:, 256 * u + P * s : 256 * u + P * s + P],
+                                words[:, k0 : k0 + P],
+                                ident[:],
+                            )
+            waiting = None
+            for c, i0, n in units:
+                wg = grp.tile([P, 2048], BF16, name="wg", tag="wg", align_bytes=64)
+                for h in range(n // 256):
+                    bank = banks.pop(0)
+                    m0 = mask_col(c, i0 + 256 * h)
+                    nc.vector.tensor_tensor(
+                        out=wg[:, 1024 * h : 1024 * h + 1024].rearrange(
+                            "q (i u e) -> q i u e", u=2, e=2
+                        ),
+                        in0=bank[:].bitcast(BF16).rearrange("q (u i e) -> q i u e", u=2, e=2),
+                        in1=m_sb[c][:, :, :, m0 : m0 + 256].rearrange("q u e i -> q i u e"),
+                        op=mybir.AluOpType.mult,
+                    )
+                    if waiting is not None:
+                        quantise_w(*waiting)
+                        waiting = None
+                waiting = (c, i0, n, wg)
+            quantise_w(*waiting)
+
         def prep_g(j, c):
-            banks = tp.tile([P, 2, 512], F32, name="gbanks", tag="tp")
+            gg = grp.tile([P, 2, 512], F32, name="gg", tag="gg", align_bytes=64)
             for h in range(2):
+                bank = tp.tile([P, 512], F32, name="gbank", tag="tp")
                 for tt in range(2):
                     words = g_sb[2 * j + h][:, tt, :].bitcast(F32)
                     for u in range(2):
                         k0 = 256 * c + P * u
                         nc.tensor.transpose(
-                            banks[:, h, 256 * u + P * tt : 256 * u + P * tt + P],
+                            bank[:, 256 * u + P * tt : 256 * u + P * tt + P],
                             words[:, k0 : k0 + P],
                             ident[:],
                         )
-            gg = grp.tile([P, 2, 512], F32, name="gg", tag="gg", align_bytes=64)
-            for h in range(2):
                 nc.scalar.copy(
                     out=gg[:, h, :].rearrange("q (j u) -> q j u", u=2),
-                    in_=banks[:, h, :].rearrange("q (u j) -> q j u", u=2),
+                    in_=bank[:].rearrange("q (u j) -> q j u", u=2),
                 )
             nc.vector.quantize_mx(
                 out=gcodes[:, c, 512 * j : 512 * j + 512].bitcast(E5X4),
@@ -188,7 +216,8 @@ def tile_gpi_t_kernel(tc, x, w, b, mask, grad_out, out):
                 in_=gg[:].rearrange("q h j -> q (h j)").bitcast(BF16),
             )
 
-        def mx(passes, t, dst):
+        def mx(name, t):
+            passes = TILES[name]
             acc = accp.tile([P, 512], F32, name="acc", tag="acc")
             for k, (c, col) in enumerate(passes):
                 nc.tensor.matmul_mx(
@@ -200,49 +229,49 @@ def tile_gpi_t_kernel(tc, x, w, b, mask, grad_out, out):
                     start=(k == 0),
                     stop=(k == len(passes) - 1),
                 )
-            nc.scalar.copy(out=dst, in_=acc[:, 0 : dst.shape[1]])
-
-        T_A = [(0, 0), (1, 0), (2, 0)]
-        T_B = [(1, 512), (2, 512)]
-        T_C = [(0, 512), (1, 768)]
-        T_D = [(0, 1024), (1, 1280), (2, 768)]
-        T_E = [(1, 1792), (2, 1280)]
+            return acc
 
         ystage = []
+        Y_COL = {"C": 0, "D": 512, "E": 1024}
 
-        prep_w(0, 768, 512)
-        prep_w(1, 768, 512)
+        prep_w([(0, 768, 512), (1, 768, 512)])
         for j in range(2):
             for c in range(3):
                 prep_g(j, c)
-            for t in range(4 * j, 4 * j + 4):
-                ys = big.tile([P, 1536], F32, name="ys%d" % t, tag="big")
-                ystage.append(ys)
-                mx(T_C, t, ys[:, 0:512])
-                nc.sync.dma_start(out=out_view[:, t, 768:1280], in_=ys[:, 0:512])
-        prep_w(0, 1280, 512)
-        prep_w(1, 1280, 512)
-        prep_w(2, 1280, 512)
-        for t in range(RT):
-            if t == 2:
-                prep_w(1, 1792, 512)
-            if t == 5:
-                prep_w(2, 1792, 512)
-            mx(T_D, t, ystage[t][:, 512:1024])
-            nc.sync.dma_start(out=out_view[:, t, 1280:1792], in_=ystage[t][:, 512:1024])
-        for t in range(RT):
-            if t == 2:
-                prep_w(2, 256, 512)
-            if t == 5:
-                prep_w(1, 512, 256)
-            mx(T_E, t, ystage[t][:, 1024:1536])
-            nc.sync.dma_start(out=out_view[:, t, 1792:2304], in_=ystage[t][:, 1024:1536])
-        for t in range(RT):
-            if t == 2:
-                prep_w(0, 0, 512)
-            if t == 5:
-                prep_w(1, 0, 512)
-            mx(T_B, t, xstage[t][:, 512:768])
-        for t in range(RT):
-            mx(T_A, t, xstage[t][:, 0:512])
-            nc.sync.dma_start(out=out_view[:, t, 0:768], in_=xstage[t][:])
+        group = 0
+        for name in TILE_ORDER:
+            for t in range(RT):
+                if group in W_BEFORE:
+                    prep_w(W_BEFORE[group])
+                group += 1
+                acc = mx(name, t)
+                if name == "X2":
+                    nc.scalar.copy(
+                        out=xstage[t][:, 0:4:3, :],
+                        in_=acc[:].rearrange("p (a i) -> p a i", a=2),
+                    )
+                elif name == "X1":
+                    nc.scalar.copy(
+                        out=xstage[t][:, 1:3, :],
+                        in_=acc[:].rearrange("p (a i) -> p a i", a=2),
+                    )
+                    nc.vector.tensor_tensor(
+                        out=xstage[t][:, 2, :],
+                        in0=xstage[t][:, 2, :],
+                        in1=xstage[t][:, 0, :],
+                        op=mybir.AluOpType.add,
+                    )
+                    nc.sync.dma_start(
+                        out=out_view[:, t, 0:768],
+                        in_=xstage[t][:, 1:4, :].rearrange("p a i -> p (a i)"),
+                    )
+                else:
+                    if name == "C":
+                        ys = big.tile([P, 1536], F32, name="ys%d" % t, tag="big")
+                        ystage.append(ys)
+                    y0 = Y_COL[name]
+                    nc.scalar.copy(out=ystage[t][:, y0 : y0 + 512], in_=acc[:])
+                    nc.sync.dma_start(
+                        out=out_view[:, t, 768 + y0 : 768 + y0 + 512],
+                        in_=ystage[t][:, y0 : y0 + 512],
+                    )

@@ -37,13 +37,13 @@ TILES = {
     "D": [(0, 1024), (1, 1536), (2, 512)],
     "X1": [(1, 0), (0, 0)],
 }
-TILE_ORDER = ["C", "X2", "E", "D", "X1"]
+TILE_ORDER = ["C", "X2", "X1", "D", "E"]
 W_BEFORE = {
-    2: [(2, 256, 512), (1, 512, 256)],
-    7: [(1, 1792, 512), (2, 1792, 512)],
+    3: [(2, 256, 512), (1, 512, 256)],
+    8: [(1, 0, 512), (0, 0, 512)],
     14: [(0, 1280, 512), (1, 1280, 512)],
-    20: [(2, 1280, 512), (1, 0, 512)],
-    24: [(0, 0, 512)],
+    19: [(2, 1280, 512)],
+    24: [(1, 1792, 512), (2, 1792, 512)],
 }
 
 
@@ -124,25 +124,24 @@ def tile_gpi_t_kernel(tc, x, w, b, mask, grad_out, out):
             nc.sync.dma_start(out=gt[:], in_=g_view[:, 2 * pair : 2 * pair + 2, :])
             g_sb.append(gt)
 
+        load_g(0)
+        load_g(1)
         load_w(3)
         load_mask(0, 768, 1280)
         load_mask(1, 768, 1280)
-        for pair in range(4):
-            load_g(pair)
+        load_g(2)
+        load_g(3)
         load_w(2)
         load_w(1)
         load_mask(2, 256, 768)
-        load_mask(1, 512, 768)
-        load_w(5)
-        load_mask(1, 1792, 2304)
-        load_mask(2, 1792, 2304)
+        load_mask(1, 0, 768)
+        load_w(0)
+        load_mask(0, 0, 512)
         load_w(4)
         load_mask(0, 1280, 1792)
-        load_mask(1, 1280, 1792)
-        load_mask(2, 1280, 1792)
-        load_w(0)
-        load_mask(1, 0, 512)
-        load_mask(0, 0, 512)
+        load_mask(1, 1280, 2304)
+        load_mask(2, 1280, 2304)
+        load_w(5)
 
         def w_words(i):
             for n, (i0, i1, u0, u1) in enumerate(BLOCKS):
@@ -234,10 +233,11 @@ def tile_gpi_t_kernel(tc, x, w, b, mask, grad_out, out):
         ystage = []
         Y_COL = {"C": 0, "D": 512, "E": 1024}
 
+        for c in range(3):
+            prep_g(0, c)
         prep_w([(0, 768, 512), (1, 768, 512)])
-        for j in range(2):
-            for c in range(3):
-                prep_g(j, c)
+        for c in range(3):
+            prep_g(1, c)
         group = 0
         for name in TILE_ORDER:
             for t in range(RT):

@@ -42,8 +42,13 @@ W_BEFORE = {
     3: [(2, 256, 512), (1, 512, 256)],
     8: [(1, 0, 512), (0, 0, 512)],
     14: [(0, 1280, 512), (1, 1280, 512)],
-    19: [(2, 1280, 512)],
+    20: [(2, 1280, 512)],
     24: [(1, 1792, 512), (2, 1792, 512)],
+}
+I_BEFORE = {
+    8: (0, 0, 512),
+    16: (2, 1280, 512),
+    24: (2, 1792, 512),
 }
 
 
@@ -67,6 +72,7 @@ def tile_gpi_t_kernel(tc, x, w, b, mask, grad_out, out):
         keep = ctx.enter_context(tc.tile_pool(name="keep", bufs=1))
         big = ctx.enter_context(tc.tile_pool(name="big", bufs=8))
         grp = ctx.enter_context(tc.tile_pool(name="grp", bufs=3))
+        two = ctx.enter_context(tc.tile_pool(name="two", bufs=2))
         tp = ctx.enter_context(tc.psum_pool(name="tp", bufs=4))
         accp = ctx.enter_context(tc.psum_pool(name="accp", bufs=4))
         ctx.enter_context(tc.manual_schedule())
@@ -157,6 +163,20 @@ def tile_gpi_t_kernel(tc, x, w, b, mask, grad_out, out):
                 in_=wg[:, 0 : 4 * n],
             )
 
+        paired = {}
+
+        def pair_mask(c, i0, n):
+            mi = two.tile([P, 2048], BF16, name="mi", tag="mi")
+            for h in range(n // 256):
+                m0 = mask_col(c, i0 + 256 * h)
+                nc.scalar.copy(
+                    out=mi[:, 1024 * h : 1024 * h + 1024].rearrange(
+                        "q (u i e) -> q u i e", u=2, e=2
+                    ),
+                    in_=m_sb[c][:, :, :, m0 : m0 + 256].rearrange("q u e i -> q u i e"),
+                )
+            paired[(c, i0)] = mi
+
         def prep_w(units):
             banks = []
             for c, i0, n in units:
@@ -178,12 +198,18 @@ def tile_gpi_t_kernel(tc, x, w, b, mask, grad_out, out):
                 for h in range(n // 256):
                     bank = banks.pop(0)
                     m0 = mask_col(c, i0 + 256 * h)
+                    if (c, i0) in paired:
+                        rows = paired[(c, i0)][:, 1024 * h : 1024 * h + 1024].rearrange(
+                            "q (u i e) -> q i u e", u=2, e=2
+                        )
+                    else:
+                        rows = m_sb[c][:, :, :, m0 : m0 + 256].rearrange("q u e i -> q i u e")
                     nc.vector.tensor_tensor(
                         out=wg[:, 1024 * h : 1024 * h + 1024].rearrange(
                             "q (i u e) -> q i u e", u=2, e=2
                         ),
                         in0=bank[:].bitcast(BF16).rearrange("q (u i e) -> q i u e", u=2, e=2),
-                        in1=m_sb[c][:, :, :, m0 : m0 + 256].rearrange("q u e i -> q i u e"),
+                        in1=rows,
                         op=mybir.AluOpType.mult,
                     )
                     if waiting is not None:
@@ -193,7 +219,7 @@ def tile_gpi_t_kernel(tc, x, w, b, mask, grad_out, out):
             quantise_w(*waiting)
 
         def prep_g(j, c):
-            gg = grp.tile([P, 2, 512], F32, name="gg", tag="gg", align_bytes=64)
+            gg = two.tile([P, 2, 512], F32, name="gg", tag="gg", align_bytes=64)
             for h in range(2):
                 bank = tp.tile([P, 512], F32, name="gbank", tag="tp")
                 for tt in range(2):
@@ -241,6 +267,8 @@ def tile_gpi_t_kernel(tc, x, w, b, mask, grad_out, out):
         group = 0
         for name in TILE_ORDER:
             for t in range(RT):
+                if group in I_BEFORE:
+                    pair_mask(*I_BEFORE[group])
                 if group in W_BEFORE:
                     prep_w(W_BEFORE[group])
                 group += 1

@@ -39,7 +39,7 @@ TILES = {
 }
 TILE_ORDER = ["C", "X2", "X1", "D", "E"]
 W_BEFORE = {
-    3: [(2, 256, 512), (1, 512, 256)],
+    2: [(2, 256, 512), (1, 512, 256)],
     8: [(1, 0, 512), (0, 0, 512)],
     14: [(0, 1280, 512), (1, 1280, 512)],
     20: [(2, 1280, 512)],
@@ -283,7 +283,7 @@ def tile_gpi_t_kernel(tc, x, w, b, mask, grad_out, out):
                         out=xstage[t][:, 1:3, :],
                         in_=acc[:].rearrange("p (a i) -> p a i", a=2),
                     )
-                    nc.vector.tensor_tensor(
+                    nc.gpsimd.tensor_tensor(
                         out=xstage[t][:, 2, :],
                         in0=xstage[t][:, 2, :],
                         in1=xstage[t][:, 0, :],

@@ -46,8 +46,9 @@ W_BEFORE = {
     24: [(1, 1792, 512), (2, 1792, 512)],
 }
 I_BEFORE = {
-    8: (0, 0, 512),
-    16: (2, 1280, 512),
+    5: (0, 0, 512),
+    14: (1, 1280, 512),
+    20: (2, 1280, 512),
     24: (2, 1792, 512),
 }
 
@@ -283,7 +284,7 @@ def tile_gpi_t_kernel(tc, x, w, b, mask, grad_out, out):
                         out=xstage[t][:, 1:3, :],
                         in_=acc[:].rearrange("p (a i) -> p a i", a=2),
                     )
-                    nc.gpsimd.tensor_tensor(
+                    nc.vector.tensor_tensor(
                         out=xstage[t][:, 2, :],
                         in0=xstage[t][:, 2, :],
                         in1=xstage[t][:, 0, :],

@@ -258,6 +258,14 @@ def tile_gpi_t_kernel(tc, x, w, b, mask, grad_out, out):
             return acc
 
         ystage = []
+        late = []
+
+        def store_y(engine, t, y0):
+            engine.dma_start(
+                out=out_view[:, t, 768 + y0 : 768 + y0 + 512],
+                in_=ystage[t][:, y0 : y0 + 512],
+            )
+
         Y_COL = {"C": 0, "D": 512, "E": 1024}
 
         for c in range(3):
@@ -280,13 +288,10 @@ def tile_gpi_t_kernel(tc, x, w, b, mask, grad_out, out):
                         in_=acc[:].rearrange("p (a i) -> p a i", a=2),
                     )
                 elif name == "X1":
-                    nc.scalar.copy(
-                        out=xstage[t][:, 1:3, :],
-                        in_=acc[:].rearrange("p (a i) -> p a i", a=2),
-                    )
+                    nc.scalar.copy(out=xstage[t][:, 1, :], in_=acc[:, 0:256])
                     nc.vector.tensor_tensor(
                         out=xstage[t][:, 2, :],
-                        in0=xstage[t][:, 2, :],
+                        in0=acc[:, 256:512],
                         in1=xstage[t][:, 0, :],
                         op=mybir.AluOpType.add,
                     )
@@ -300,7 +305,12 @@ def tile_gpi_t_kernel(tc, x, w, b, mask, grad_out, out):
                         ystage.append(ys)
                     y0 = Y_COL[name]
                     nc.scalar.copy(out=ystage[t][:, y0 : y0 + 512], in_=acc[:])
-                    nc.sync.dma_start(
-                        out=out_view[:, t, 768 + y0 : 768 + y0 + 512],
-                        in_=ystage[t][:, y0 : y0 + 512],
-                    )
+                    for tt, c0 in late:
+                        store_y(nc.scalar, tt, c0)
+                    late.clear()
+                    if name != "C" and t % 2 == 1:
+                        late.append((t, y0))
+                    else:
+                        store_y(nc.sync, t, y0)
+        for tt, c0 in late:
+            store_y(nc.scalar, tt, c0)

@@ -71,7 +71,7 @@ def tile_gpi_t_kernel(tc, x, w, b, mask, grad_out, out):
     nc = tc.nc
     with ExitStack() as ctx:
         keep = ctx.enter_context(tc.tile_pool(name="keep", bufs=1))
-        big = ctx.enter_context(tc.tile_pool(name="big", bufs=8))
+        big = ctx.enter_context(tc.tile_pool(name="big", bufs=4))
         grp = ctx.enter_context(tc.tile_pool(name="grp", bufs=3))
         two = ctx.enter_context(tc.tile_pool(name="two", bufs=2))
         tp = ctx.enter_context(tc.psum_pool(name="tp", bufs=4))
@@ -100,7 +100,8 @@ def tile_gpi_t_kernel(tc, x, w, b, mask, grad_out, out):
         gcodes = keep.tile([P, 3, ROWS], U32, name="gcodes", tag="gcodes", align_bytes=64)
         gscales = keep.tile([P, 3, ROWS], U8, name="gscales", tag="gscales", align_bytes=64)
         xstage = [
-            keep.tile([P, 4, 256], F32, name="xs%d" % t, tag="xs%d" % t) for t in range(RT)
+            keep.tile([P, 2, 4, 256], F32, name="xs%d" % n, tag="xs%d" % n)
+            for n in range(RT // 2)
         ]
 
         nc.vector.memset(wcodes[1][:, 512:768].bitcast(I32), 0)
@@ -127,9 +128,14 @@ def tile_gpi_t_kernel(tc, x, w, b, mask, grad_out, out):
         g_sb = []
 
         def load_g(pair):
-            gt = big.tile([P, 2, UNITS], BF16, name="g%d" % pair, tag="big")
-            nc.sync.dma_start(out=gt[:], in_=g_view[:, 2 * pair : 2 * pair + 2, :])
-            g_sb.append(gt)
+            if pair % 2 == 0:
+                gt = big.tile([P, 4, UNITS], BF16, name="g%d" % pair, tag="big")
+                g_sb.append(gt)
+            t0 = 2 * (pair % 2)
+            nc.sync.dma_start(
+                out=g_sb[pair // 2][:, t0 : t0 + 2, :],
+                in_=g_view[:, 2 * pair : 2 * pair + 2, :],
+            )
 
         load_g(0)
         load_g(1)
@@ -224,7 +230,7 @@ def tile_gpi_t_kernel(tc, x, w, b, mask, grad_out, out):
             for h in range(2):
                 bank = tp.tile([P, 512], F32, name="gbank", tag="tp")
                 for tt in range(2):
-                    words = g_sb[2 * j + h][:, tt, :].bitcast(F32)
+                    words = g_sb[j][:, 2 * h + tt, :].bitcast(F32)
                     for u in range(2):
                         k0 = 256 * c + P * u
                         nc.tensor.transpose(
@@ -260,10 +266,10 @@ def tile_gpi_t_kernel(tc, x, w, b, mask, grad_out, out):
         ystage = []
         late = []
 
-        def store_y(engine, t, y0):
+        def store_y(engine, t0, t1, y0):
             engine.dma_start(
-                out=out_view[:, t, 768 + y0 : 768 + y0 + 512],
-                in_=ystage[t][:, y0 : y0 + 512],
+                out=out_view[:, t0:t1, 768 + y0 : 768 + y0 + 512],
+                in_=ystage[t0 // 2][:, t0 % 2 : t0 % 2 + t1 - t0, y0 : y0 + 512],
             )
 
         Y_COL = {"C": 0, "D": 512, "E": 1024}
@@ -284,33 +290,35 @@ def tile_gpi_t_kernel(tc, x, w, b, mask, grad_out, out):
                 acc = mx(name, t)
                 if name == "X2":
                     nc.scalar.copy(
-                        out=xstage[t][:, 0:4:3, :],
+                        out=xstage[t // 2][:, t % 2, 0:4:3, :],
                         in_=acc[:].rearrange("p (a i) -> p a i", a=2),
                     )
                 elif name == "X1":
-                    nc.scalar.copy(out=xstage[t][:, 1, :], in_=acc[:, 0:256])
+                    xs = xstage[t // 2][:, t % 2]
+                    nc.scalar.copy(out=xs[:, 1, :], in_=acc[:, 0:256])
                     nc.vector.tensor_tensor(
-                        out=xstage[t][:, 2, :],
+                        out=xs[:, 2, :],
                         in0=acc[:, 256:512],
-                        in1=xstage[t][:, 0, :],
+                        in1=xs[:, 0, :],
                         op=mybir.AluOpType.add,
                     )
-                    nc.sync.dma_start(
-                        out=out_view[:, t, 0:768],
-                        in_=xstage[t][:, 1:4, :].rearrange("p a i -> p (a i)"),
-                    )
+                    if t % 2 == 1:
+                        nc.sync.dma_start(
+                            out=out_view[:, t - 1 : t + 1, 0:768],
+                            in_=xstage[t // 2][:, :, 1:4, :].rearrange("p t a i -> p t (a i)"),
+                        )
                 else:
-                    if name == "C":
-                        ys = big.tile([P, 1536], F32, name="ys%d" % t, tag="big")
+                    if name == "C" and t % 2 == 0:
+                        ys = big.tile([P, 2, 1536], F32, name="ys%d" % t, tag="big")
                         ystage.append(ys)
                     y0 = Y_COL[name]
-                    nc.scalar.copy(out=ystage[t][:, y0 : y0 + 512], in_=acc[:])
-                    for tt, c0 in late:
-                        store_y(nc.scalar, tt, c0)
+                    nc.scalar.copy(out=ystage[t // 2][:, t % 2, y0 : y0 + 512], in_=acc[:])
+                    for stored in late:
+                        store_y(nc.scalar, *stored)
                     late.clear()
-                    if name != "C" and t % 2 == 1:
-                        late.append((t, y0))
-                    else:
-                        store_y(nc.sync, t, y0)
-        for tt, c0 in late:
-            store_y(nc.scalar, tt, c0)
+                    if name == "E" and t >= RT - 2:
+                        store_y(nc.sync, t, t + 1, y0)
+                    elif t % 4 == 3 and name != "C":
+                        late.append((t - 1, t + 1, y0))
+                    elif t % 2 == 1:
+                        store_y(nc.sync, t - 1, t + 1, y0)

from contextlib import ExitStack

import concourse.masks as masks
import concourse.mybir as mybir

BF16 = mybir.dt.bfloat16
F32 = mybir.dt.float32
I32 = mybir.dt.int32
U32 = mybir.dt.uint32
U8 = mybir.dt.uint8
E4X4 = mybir.dt.float8_e4m3fn_x4
E5X4 = mybir.dt.float8_e5m2_x4

P = 128
ROWS = 1024
UNITS = 1536
INPUTS = 2304
RT = ROWS // P
FLOPS = 2 * ROWS * 2752512
BYTES = 2 * ROWS * UNITS + 2 * 2 * 2752512 + 4 * ROWS * INPUTS

BLOCKS = [
    (0, 256, 0, 1024),
    (256, 512, 0, 1536),
    (512, 768, 512, 1536),
    (768, 1280, 0, 1024),
    (1280, 1792, 0, 1536),
    (1792, 2304, 512, 1536),
]
MASK_W = [1536, 2304, 1536]
CODE_W = [1536, 2560, 1536]

TILES = {
    "C": [(0, 512), (1, 1024)],
    "X2": [(1, 512), (2, 0)],
    "E": [(1, 2048), (2, 1024)],
    "D": [(0, 1024), (1, 1536), (2, 512)],
    "X1": [(1, 0), (0, 0)],
}
TILE_ORDER = ["C", "X2", "X1", "D", "E"]
W_BEFORE = {
    2: [(2, 256, 512), (1, 512, 256)],
    8: [(1, 0, 512), (0, 0, 512)],
    14: [(0, 1280, 512), (1, 1280, 512)],
    20: [(2, 1280, 512)],
    24: [(1, 1792, 512), (2, 1792, 512)],
}
I_BEFORE = {
    5: (0, 0, 512),
    14: (1, 1280, 512),
    20: (2, 1280, 512),
    24: (2, 1792, 512),
}


def mask_col(c, i):
    if c == 0:
        return i if i < 512 else i - 256
    if c == 1:
        return i
    return i - 256 if i < 768 else i - 768


def code_col(c, i):
    if c == 1:
        return i if i < 512 else i + 256
    return mask_col(c, i)


def tile_gpi_t_kernel(tc, x, w, b, mask, grad_out, out):
    nc = tc.nc
    with ExitStack() as ctx:
        keep = ctx.enter_context(tc.tile_pool(name="keep", bufs=1))
        big = ctx.enter_context(tc.tile_pool(name="big", bufs=4))
        grp = ctx.enter_context(tc.tile_pool(name="grp", bufs=3))
        two = ctx.enter_context(tc.tile_pool(name="two", bufs=2))
        tp = ctx.enter_context(tc.psum_pool(name="tp", bufs=4))
        accp = ctx.enter_context(tc.psum_pool(name="accp", bufs=4))
        ctx.enter_context(tc.manual_schedule())

        ident = keep.tile([P, P], F32, name="ident", tag="ident")
        masks.make_identity(nc, ident[:])

        w_sb = [
            keep.tile([P, (i1 - i0) // P, u1 - u0], BF16, name="w%d" % n, tag="w%d" % n)
            for n, (i0, i1, u0, u1) in enumerate(BLOCKS)
        ]
        m_sb = [
            keep.tile([P, 2, 2, MASK_W[c]], BF16, name="m%d" % c, tag="m%d" % c)
            for c in range(3)
        ]
        wcodes = [
            keep.tile([P, CODE_W[c]], U32, name="wc%d" % c, tag="wc%d" % c, align_bytes=64)
            for c in range(3)
        ]
        wscales = [
            keep.tile([P, CODE_W[c]], U8, name="ws%d" % c, tag="ws%d" % c, align_bytes=64)
            for c in range(3)
        ]
        gcodes = keep.tile([P, 3, ROWS], U32, name="gcodes", tag="gcodes", align_bytes=64)
        gscales = keep.tile([P, 3, ROWS], U8, name="gscales", tag="gscales", align_bytes=64)
        xstage = [
            keep.tile([P, 2, 4, 256], F32, name="xs%d" % n, tag="xs%d" % n)
            for n in range(RT // 2)
        ]

        nc.vector.memset(wcodes[1][:, 512:768].bitcast(I32), 0)
        nc.vector.memset(wscales[1][:, 512:768].bitcast(I32), 0)

        g_view = grad_out.rearrange("(p t) u -> p t u", t=RT)
        out_view = out.rearrange("(p t) i -> p t i", t=RT)

        def load_w(n):
            i0, i1, u0, u1 = BLOCKS[n]
            nc.sync.dma_start(
                out=w_sb[n][:], in_=w[i0:i1, u0:u1].rearrange("(s p) u -> p s u", p=P)
            )

        def load_mask(c, i0, i1):
            m0 = mask_col(c, i0)
            for u in range(2):
                r0 = 512 * c + 256 * u
                nc.sync.dma_start(
                    out=m_sb[c][:, u, :, m0 : m0 + i1 - i0],
                    in_=mask[r0 : r0 + 256, i0:i1].rearrange("(q e) i -> q e i", e=2),
                )

        g_sb = []

        def load_g(pair):
            if pair % 2 == 0:
                gt = big.tile([P, 4, UNITS], BF16, name="g%d" % pair, tag="big")
                g_sb.append(gt)
            t0 = 2 * (pair % 2)
            nc.sync.dma_start(
                out=g_sb[pair // 2][:, t0 : t0 + 2, :],
                in_=g_view[:, 2 * pair : 2 * pair + 2, :],
            )

        load_g(0)
        load_g(1)
        load_w(3)
        load_mask(0, 768, 1280)
        load_mask(1, 768, 1280)
        load_g(2)
        load_g(3)
        load_w(2)
        load_w(1)
        load_mask(2, 256, 768)
        load_mask(1, 0, 768)
        load_w(0)
        load_mask(0, 0, 512)
        load_w(4)
        load_mask(0, 1280, 1792)
        load_mask(1, 1280, 2304)
        load_mask(2, 1280, 2304)
        load_w(5)

        def w_words(i):
            for n, (i0, i1, u0, u1) in enumerate(BLOCKS):
                if i0 <= i < i1:
                    return w_sb[n][:, (i - i0) // P, :].bitcast(F32), u0 // 2
            raise ValueError("no block")

        def quantise_w(c, i0, n, wg):
            c0 = code_col(c, i0)
            nc.vector.quantize_mx(
                out=wcodes[c][:, c0 : c0 + n].bitcast(E4X4),
                scales=wscales[c][:, c0 : c0 + n],
                in_=wg[:, 0 : 4 * n],
            )

        paired = {}

        def pair_mask(c, i0, n):
            mi = two.tile([P, 2048], BF16, name="mi", tag="mi")
            for h in range(n // 256):
                m0 = mask_col(c, i0 + 256 * h)
                nc.scalar.copy(
                    out=mi[:, 1024 * h : 1024 * h + 1024].rearrange(
                        "q (u i e) -> q u i e", u=2, e=2
                    ),
                    in_=m_sb[c][:, :, :, m0 : m0 + 256].rearrange("q u e i -> q u i e"),
                )
            paired[(c, i0)] = mi

        def prep_w(units):
            banks = []
            for c, i0, n in units:
                for h in range(n // 256):
                    bank = tp.tile([P, 512], F32, name="wbank", tag="tp")
                    banks.append(bank)
                    for s in range(2):
                        words, first = w_words(i0 + 256 * h + P * s)
                        for u in range(2):
                            k0 = 256 * c + P * u - first
                            nc.tensor.transpose(
                                bank[:, 256 * u + P * s : 256 * u + P * s + P],
                                words[:, k0 : k0 + P],
                                ident[:],
                            )
            waiting = None
            for c, i0, n in units:
                wg = grp.tile([P, 2048], BF16, name="wg", tag="wg", align_bytes=64)
                for h in range(n // 256):
                    bank = banks.pop(0)
                    m0 = mask_col(c, i0 + 256 * h)
                    if (c, i0) in paired:
                        rows = paired[(c, i0)][:, 1024 * h : 1024 * h + 1024].rearrange(
                            "q (u i e) -> q i u e", u=2, e=2
                        )
                    else:
                        rows = m_sb[c][:, :, :, m0 : m0 + 256].rearrange("q u e i -> q i u e")
                    nc.vector.tensor_tensor(
                        out=wg[:, 1024 * h : 1024 * h + 1024].rearrange(
                            "q (i u e) -> q i u e", u=2, e=2
                        ),
                        in0=bank[:].bitcast(BF16).rearrange("q (u i e) -> q i u e", u=2, e=2),
                        in1=rows,
                        op=mybir.AluOpType.mult,
                    )
                    if waiting is not None:
                        quantise_w(*waiting)
                        waiting = None
                waiting = (c, i0, n, wg)
            quantise_w(*waiting)

        def prep_g(j, c):
            gg = two.tile([P, 2, 512], F32, name="gg", tag="gg", align_bytes=64)
            for h in range(2):
                bank = tp.tile([P, 512], F32, name="gbank", tag="tp")
                for tt in range(2):
                    words = g_sb[j][:, 2 * h + tt, :].bitcast(F32)
                    for u in range(2):
                        k0 = 256 * c + P * u
                        nc.tensor.transpose(
                            bank[:, 256 * u + P * tt : 256 * u + P * tt + P],
                            words[:, k0 : k0 + P],
                            ident[:],
                        )
                nc.scalar.copy(
                    out=gg[:, h, :].rearrange("q (j u) -> q j u", u=2),
                    in_=bank[:].rearrange("q (u j) -> q j u", u=2),
                )
            nc.vector.quantize_mx(
                out=gcodes[:, c, 512 * j : 512 * j + 512].bitcast(E5X4),
                scales=gscales[:, c, 512 * j : 512 * j + 512],
                in_=gg[:].rearrange("q h j -> q (h j)").bitcast(BF16),
            )

        def mx(name, t):
            passes = TILES[name]
            acc = accp.tile([P, 512], F32, name="acc", tag="acc")
            for k, (c, col) in enumerate(passes):
                nc.tensor.matmul_mx(
                    out=acc[:],
                    lhsT=gcodes[:, c, P * t : P * t + P].bitcast(E5X4),
                    lhsT_scale=gscales[:, c, P * t : P * t + P],
                    rhs=wcodes[c][:, col : col + 512].bitcast(E4X4),
                    rhs_scale=wscales[c][:, col : col + 512],
                    start=(k == 0),
                    stop=(k == len(passes) - 1),
                )
            return acc

        ystage = []
        late = []

        def store_y(engine, t0, t1, y0):
            engine.dma_start(
                out=out_view[:, t0:t1, 768 + y0 : 768 + y0 + 512],
                in_=ystage[t0 // 2][:, t0 % 2 : t0 % 2 + t1 - t0, y0 : y0 + 512],
            )

        Y_COL = {"C": 0, "D": 512, "E": 1024}

        for c in range(3):
            prep_g(0, c)
        prep_w([(0, 768, 512), (1, 768, 512)])
        for c in range(3):
            prep_g(1, c)
        group = 0
        for name in TILE_ORDER:
            for t in range(RT):
                if group in I_BEFORE:
                    pair_mask(*I_BEFORE[group])
                if group in W_BEFORE:
                    prep_w(W_BEFORE[group])
                group += 1
                acc = mx(name, t)
                if name == "X2":
                    nc.scalar.copy(
                        out=xstage[t // 2][:, t % 2, 0:4:3, :],
                        in_=acc[:].rearrange("p (a i) -> p a i", a=2),
                    )
                elif name == "X1":
                    xs = xstage[t // 2][:, t % 2]
                    nc.scalar.copy(out=xs[:, 1, :], in_=acc[:, 0:256])
                    nc.vector.tensor_tensor(
                        out=xs[:, 2, :],
                        in0=acc[:, 256:512],
                        in1=xs[:, 0, :],
                        op=mybir.AluOpType.add,
                    )
                    if t % 2 == 1:
                        nc.sync.dma_start(
                            out=out_view[:, t - 1 : t + 1, 0:768],
                            in_=xstage[t // 2][:, :, 1:4, :].rearrange("p t a i -> p t (a i)"),
                        )
                else:
                    if name == "C" and t % 2 == 0:
                        ys = big.tile([P, 2, 1536], F32, name="ys%d" % t, tag="big")
                        ystage.append(ys)
                    y0 = Y_COL[name]
                    nc.scalar.copy(out=ystage[t // 2][:, t % 2, y0 : y0 + 512], in_=acc[:])
                    for stored in late:
                        store_y(nc.scalar, *stored)
                    late.clear()
                    if name == "E" and t >= RT - 2:
                        store_y(nc.sync, t, t + 1, y0)
                    elif t % 4 == 3 and name != "C":
                        late.append((t - 1, t + 1, y0))
                    elif t % 2 == 1:
                        store_y(nc.sync, t - 1, t + 1, y0)
